import numpy as np
import ml_dtypes


def mxq(x, axis, fmt="e4m3"):
    dtype, down = {"e4m3": (ml_dtypes.float8_e4m3fn, 7), "e5m2": (ml_dtypes.float8_e5m2, 14)}[fmt]
    v = np.moveaxis(np.asarray(x, np.float32).astype(ml_dtypes.bfloat16).astype(np.float64), axis, -1)
    blocks = v.reshape(v.shape[:-1] + (-1, 32))
    amax = np.abs(blocks).max(-1, keepdims=True)
    byte = np.maximum(np.where(amax > 0, np.frexp(amax)[1] - 1 + 127, 0) - down, 1)
    scale = np.exp2(byte - 127.0)
    codes = (blocks / scale).astype(np.float32).astype(dtype).astype(np.float64)
    return np.moveaxis((codes * scale).reshape(v.shape), -1, axis)


WIDE = False


def mx_kscale(k):
    if not WIDE:
        return np.ones(k)
    levels = np.array([10, -10, 5, -5, 0])
    if k % 512:
        return np.exp2(np.random.permutation(np.resize(levels, k // 32))).repeat(32)
    a = np.empty((k // 512, 16))
    for p in range(k // 512):
        a[p, :8] = np.random.permutation(np.resize(levels, 8))
        for g in range(8):
            far = levels[np.abs(levels - a[p, g]) >= 10]
            a[p, g + 8] = far[np.random.randint(len(far))]
    return np.exp2(a.ravel()).repeat(32)


BF16 = ml_dtypes.bfloat16


def bf(x):
    return np.asarray(x, np.float32).astype(BF16)


def f64(x):
    return np.asarray(x).astype(np.float64)


B, S, D, DV, NS, SD = 4, 128, 1024, 1024, 4, 256
R = B * S


def silu(v):
    return v / (1.0 + np.exp(-v))


def setup_inputs():
    s, r, t = mx_kscale(D), mx_kscale(D), mx_kscale(DV)
    return {"x": bf(np.random.standard_normal((B, S, D)) * r),
            "h": bf(np.random.standard_normal((B, S, D)) * s),
            "Wv": bf(np.random.standard_normal((NS, DV, D)) / np.sqrt(D) * t[:, None] / s),
            "W1": bf(np.random.standard_normal((NS, SD, D + DV)) / np.sqrt(D + DV) / np.concatenate([r, t]))}


def reference(x, h, Wv, W1):
    xf = f64(x).reshape(R, D)
    hf = f64(h).reshape(R, D)
    w1 = f64(W1)
    views = mxq(hf, 1, "e4m3") @ mxq(f64(Wv).transpose(0, 2, 1), 1, "e4m3")
    a = mxq(xf, 1, "e4m3") @ mxq(w1[:, :, :D].transpose(0, 2, 1), 1, "e4m3")
    b = mxq(views, 2, "e4m3") @ mxq(w1[:, :, D:].transpose(0, 2, 1), 1, "e4m3")
    return silu(a + b).reshape(NS, B, S, SD)

@@ -1,0 +1,232 @@
+from contextlib import ExitStack
+
+import concourse.mybir as mybir
+from concourse.masks import make_identity
+
+F32 = mybir.dt.float32
+BF16 = mybir.dt.bfloat16
+U32 = mybir.dt.uint32
+U8 = mybir.dt.uint8
+FP8X4 = mybir.dt.float8_e4m3fn_x4
+SILU = mybir.ActivationFunctionType.Silu
+
+P = 128
+NS = 4
+R = 512
+D = 1024
+DV = 1024
+SD = 256
+FLOPS = 2 * NS * R * (D * DV + (D + DV) * SD)
+
+
+def tile_distributedb_pa_kernel(tc, x, h, Wv, W1, out):
+    nc = tc.nc
+    with ExitStack() as ctx:
+        const = ctx.enter_context(tc.tile_pool(name="const", bufs=1))
+        inputs = ctx.enter_context(tc.tile_pool(name="inputs", bufs=1))
+        stage = ctx.enter_context(tc.tile_pool(name="stage", bufs=3))
+        keep = ctx.enter_context(tc.tile_pool(name="keep", bufs=1))
+        pair = ctx.enter_context(tc.tile_pool(name="pair", bufs=2))
+        psum = ctx.enter_context(tc.psum_pool(name="psum", bufs=8))
+        ctx.enter_context(tc.manual_schedule())
+
+        h_sb = inputs.tile([P, 4 * D], BF16, name="h_sb")
+        x_sb = inputs.tile([P, 4 * D], BF16, name="x_sb")
+        wv_sb = [inputs.tile([P, 8 * D], BF16, name="wv_sb%d" % s) for s in range(NS)]
+        w1_sb = [inputs.tile([P, 2 * (D + DV)], BF16, name="w1_sb%d" % s) for s in range(NS)]
+
+        def load_rows(dst, src):
+            view = src.flatten_outer_dims().rearrange("(m j) d -> m (j d)", j=4)
+            for half in range(2):
+                cols = slice(2 * D * half, 2 * D * (half + 1))
+                nc.sync.dma_start(out=dst[:, cols], in_=view[:, cols])
+
+        def load_wv(s, gp):
+            for u in range(2):
+                tile0 = 4 * gp + 2 * u
+                nc.sync.dma_start(
+                    out=wv_sb[s][:, tile0 * D : (tile0 + 2) * D],
+                    in_=Wv[s, 512 * gp : 512 * (gp + 1), :].rearrange("(m t) d -> m (t d)", t=4)[
+                        :, 2 * D * u : 2 * D * (u + 1)
+                    ],
+                )
+
+        def load_w1(s):
+            nc.sync.dma_start(
+                out=w1_sb[s][:].rearrange("m (a k) -> m a k", a=2),
+                in_=W1[s].rearrange("(a m) k -> m a k", a=2),
+            )
+
+        load_rows(h_sb, h)
+        load_wv(0, 0)
+        load_wv(0, 1)
+        load_w1(0)
+        load_rows(x_sb, x)
+        for s in range(1, NS):
+            load_wv(s, 0)
+            load_wv(s, 1)
+            load_w1(s)
+
+        ident = const.tile([P, P], F32, name="ident")
+        make_identity(nc, ident[:])
+        zero = const.tile([P, 1], F32, name="zero")
+        nc.vector.memset(zero[:], 0.0)
+        warm = const.tile([P, 1], F32, name="warm")
+        nc.scalar.activation(out=warm[:], in_=zero[:], func=SILU)
+
+        def copy_out(engine, dst, src):
+            if engine == "V":
+                nc.vector.tensor_copy(out=dst, in_=src)
+            else:
+                nc.scalar.copy(out=dst, in_=src)
+
+        def flush(late):
+            if late is not None:
+                late()
+
+        def transpose_round(src, tile_words, banks, codes, scales, engines, late):
+            words = src[:].bitcast(F32)
+            grouped = stage.tile([P, 4096], BF16, tag="grouped", align_bytes=64)
+            grouped_words = grouped[:].bitcast(F32)
+            for n, (slot, first_tile, k_pass) in enumerate(banks):
+                bank = psum.tile([P, 512], F32, tag="bank")
+                for u in range(2):
+                    for i in range(2):
+                        w0 = (first_tile + i) * tile_words + 256 * k_pass
+                        c0 = 256 * u + 128 * i
+                        nc.tensor.transpose(bank[:, c0 : c0 + 128], words[:, w0 + u : w0 + 256 : 2], ident[:])
+                copy_out(
+                    engines[n],
+                    grouped_words[:, 512 * slot : 512 * (slot + 1)].rearrange("p (c u) -> p c u", u=2),
+                    bank[:].rearrange("p (u c) -> p c u", u=2),
+                )
+                if n == 0:
+                    flush(late)
+            return lambda: nc.vector.quantize_mx(
+                out=codes[:].bitcast(FP8X4), scales=scales[:], in_=grouped[:]
+            )
+
+        def four_tiles(tile0):
+            return [(0, tile0, 0), (2, tile0, 1), (1, tile0 + 2, 0), (3, tile0 + 2, 1)]
+
+        h_codes = keep.tile([P, 1024], U32, name="h_codes", align_bytes=64)
+        h_scales = keep.tile([P, 1024], U8, name="h_scales", align_bytes=64)
+        x_codes = keep.tile([P, 1024], U32, name="x_codes", align_bytes=64)
+        x_scales = keep.tile([P, 1024], U8, name="x_scales", align_bytes=64)
+        wv_q = {}
+        w1_q = {}
+        views_q = {}
+
+        def wv_round(s, gp, engines, late):
+            wv_codes = pair.tile([P, 1024], U32, tag="wv_codes%d" % gp, align_bytes=64)
+            wv_scales = pair.tile([P, 1024], U8, tag="wv_scales%d" % gp, align_bytes=64)
+            wv_q[(s, gp)] = (wv_codes, wv_scales)
+            return transpose_round(wv_sb[s], 512, four_tiles(4 * gp), wv_codes, wv_scales, engines, late)
+
+        def w1_round(s, engines, late):
+            w1_codes = pair.tile([P, 1024], U32, tag="w1_codes", align_bytes=64)
+            w1_scales = pair.tile([P, 1024], U8, tag="w1_scales", align_bytes=64)
+            w1_q[s] = (w1_codes, w1_scales)
+            banks = [(n, 0, n) for n in range(4)]
+            return transpose_round(w1_sb[s], 1024, banks, w1_codes, w1_scales, engines, late)
+
+        def views_round(s, gp, engines, late, fine):
+            wv_codes, wv_scales = wv_q[(s, gp)]
+            v_grouped = pair.tile([P, 2048], BF16, tag="v_grouped%d" % gp, align_bytes=64)
+            v_codes = pair.tile([P, 512], U32, tag="v_codes%d" % gp, align_bytes=64)
+            v_scales = pair.tile([P, 512], U8, tag="v_scales%d" % gp, align_bytes=64)
+            views_q[(s, gp)] = (v_codes, v_scales)
+
+            def quantise(j0, j1):
+                nc.vector.quantize_mx(
+                    out=v_codes[:, 128 * j0 : 128 * j1].bitcast(FP8X4),
+                    scales=v_scales[:, 128 * j0 : 128 * j1],
+                    in_=v_grouped[:, 512 * j0 : 512 * j1],
+                )
+
+            for j in range(4):
+                bank = psum.tile([P, 512], F32, tag="bank")
+                for t in range(4):
+                    for g in range(2):
+                        wc = slice(512 * g + 128 * t, 512 * g + 128 * (t + 1))
+                        hc = slice(512 * g + 128 * j, 512 * g + 128 * (j + 1))
+                        nc.tensor.matmul_mx(
+                            out=bank[:, 128 * t : 128 * (t + 1)],
+                            lhsT=wv_codes[:, wc].bitcast(FP8X4),
+                            lhsT_scale=wv_scales[:, wc],
+                            rhs=h_codes[:, hc].bitcast(FP8X4),
+                            rhs_scale=h_scales[:, hc],
+                            start=(g == 0),
+                            stop=(g == 1),
+                        )
+                copy_out(
+                    engines[j],
+                    v_grouped[:, 512 * j : 512 * (j + 1)].rearrange("p (c t) -> p c t", t=4),
+                    bank[:].rearrange("p (t c) -> p c t", t=4),
+                )
+                if j == 0:
+                    flush(late)
+                if fine and j > 0:
+                    quantise(j - 1, j)
+            if fine:
+                quantise(3, 4)
+                return None
+            return lambda: quantise(0, 4)
+
+        def out_round(s, late, fine):
+            w1_codes, w1_scales = w1_q[s]
+            o_sb = pair.tile([P, 4 * SD], F32, tag="o_sb")
+            o_view = out[s].rearrange("b q f -> (b q) f").rearrange("(m j) f -> m (j f)", j=4)
+            bank = None
+            for j in range(4):
+                if fine or j % 2 == 0:
+                    bank = psum.tile([P, 512], F32, tag="bank")
+                c0 = 0 if fine else 256 * (j % 2)
+                operands = [(x_codes, x_scales, 512 * g + 128 * j) for g in range(2)]
+                operands.extend([views_q[(s, gp)] + (128 * j,) for gp in range(2)])
+                for n, (codes, scales, col) in enumerate(operands):
+                    nc.tensor.matmul_mx(
+                        out=bank[:, c0 : c0 + 256],
+                        lhsT=codes[:, col : col + 128].bitcast(FP8X4),
+                        lhsT_scale=scales[:, col : col + 128],
+                        rhs=w1_codes[:, 256 * n : 256 * (n + 1)].bitcast(FP8X4),
+                        rhs_scale=w1_scales[:, 256 * n : 256 * (n + 1)],
+                        start=(n == 0),
+                        stop=(n == 3),
+                    )
+                if fine:
+                    cols = slice(256 * j, 256 * (j + 1))
+                    nc.scalar.activation(out=o_sb[:, cols], in_=bank[:, 0:256], func=SILU)
+                    nc.sync.dma_start(out=o_view[:, cols], in_=o_sb[:, cols])
+                elif j % 2 == 1:
+                    cols = slice(256 * (j - 1), 256 * (j + 1))
+                    nc.scalar.activation(out=o_sb[:, cols], in_=bank[:], func=SILU)
+                if j == 1:
+                    flush(late)
+            if not fine:
+                nc.sync.dma_start(out=o_view, in_=o_sb[:])
+            return None
+
+        T_ENG = "VSSS"
+        V_ENG = "VSVS"
+        flush(transpose_round(h_sb, 512, four_tiles(0), h_codes, h_scales, "VSVS", None))
+        flush(wv_round(0, 0, "VSVS", None))
+        late = wv_round(0, 1, "VSVS", None)
+        late = views_round(0, 0, V_ENG, late, False)
+        late = views_round(0, 1, V_ENG, late, False)
+        late = w1_round(0, T_ENG, late)
+        late = transpose_round(x_sb, 512, four_tiles(0), x_codes, x_scales, T_ENG, late)
+        for s in range(1, NS):
+            if s > 1:
+                late = w1_round(s - 1, T_ENG, late)
+            late = wv_round(s, 0, T_ENG, late)
+            late = wv_round(s, 1, T_ENG, late)
+            if s == NS - 1:
+                late = w1_round(s, T_ENG, late)
+            late = out_round(s - 1, late, False)
+            late = views_round(s, 0, V_ENG, late, False)
+            if s < NS - 1:
+                late = views_round(s, 1, V_ENG, late, False)
+            else:
+                views_round(s, 1, "SSSV", late, True)
+        out_round(NS - 1, None, True)

@@ -26,6 +26,7 @@ def tile_distributedb_pa_kernel(tc, x, h, Wv, W1, out):
         inputs = ctx.enter_context(tc.tile_pool(name="inputs", bufs=1))
         stage = ctx.enter_context(tc.tile_pool(name="stage", bufs=3))
         keep = ctx.enter_context(tc.tile_pool(name="keep", bufs=1))
+        ordered = ctx.enter_context(tc.tile_pool(name="ordered", bufs=2))
         pair = ctx.enter_context(tc.tile_pool(name="pair", bufs=2))
         psum = ctx.enter_context(tc.psum_pool(name="psum", bufs=8))
         ctx.enter_context(tc.manual_schedule())
@@ -84,8 +85,16 @@ def tile_distributedb_pa_kernel(tc, x, h, Wv, W1, out):
             if late is not None:
                 late()
 
-        def transpose_round(src, tile_words, banks, codes, scales, engines, late):
-            words = src[:].bitcast(F32)
+        def reorder(src):
+            dst = ordered.tile([P, 4096], BF16, tag="dst", align_bytes=64)
+            nc.vector.tensor_copy(
+                out=dst[:].bitcast(F32).rearrange("p (b u w) -> p b u w", u=2, w=128),
+                in_=src.bitcast(F32).rearrange("p (b w u) -> p b u w", u=2, w=128),
+            )
+            return dst
+
+        def transpose_round(src, step, tile_words, banks, codes, scales, engines, late):
+            words = src.bitcast(F32)
             grouped = stage.tile([P, 4096], BF16, tag="grouped", align_bytes=64)
             grouped_words = grouped[:].bitcast(F32)
             for n, (slot, first_tile, k_pass) in enumerate(banks):
@@ -94,7 +103,11 @@ def tile_distributedb_pa_kernel(tc, x, h, Wv, W1, out):
                     for i in range(2):
                         w0 = (first_tile + i) * tile_words + 256 * k_pass
                         c0 = 256 * u + 128 * i
-                        nc.tensor.transpose(bank[:, c0 : c0 + 128], words[:, w0 + u : w0 + 256 : 2], ident[:])
+                        if step == 2:
+                            cols = slice(w0 + u, w0 + 256, 2)
+                        else:
+                            cols = slice(w0 + 128 * u, w0 + 128 * (u + 1))
+                        nc.tensor.transpose(bank[:, c0 : c0 + 128], words[:, cols], ident[:])
                 copy_out(
                     engines[n],
                     grouped_words[:, 512 * slot : 512 * (slot + 1)].rearrange("p (c u) -> p c u", u=2),
@@ -106,8 +119,7 @@ def tile_distributedb_pa_kernel(tc, x, h, Wv, W1, out):
                 out=codes[:].bitcast(FP8X4), scales=scales[:], in_=grouped[:]
             )
 
-        def four_tiles(tile0):
-            return [(0, tile0, 0), (2, tile0, 1), (1, tile0 + 2, 0), (3, tile0 + 2, 1)]
+        four_tiles = [(0, 0, 0), (2, 0, 1), (1, 2, 0), (3, 2, 1)]
 
         h_codes = keep.tile([P, 1024], U32, name="h_codes", align_bytes=64)
         h_scales = keep.tile([P, 1024], U8, name="h_scales", align_bytes=64)
@@ -117,18 +129,21 @@ def tile_distributedb_pa_kernel(tc, x, h, Wv, W1, out):
         w1_q = {}
         views_q = {}
 
-        def wv_round(s, gp, engines, late):
+        def wv_source(s, gp):
+            return wv_sb[s][:, 4 * D * gp : 4 * D * (gp + 1)]
+
+        def wv_round(s, gp, src, step, engines, late):
             wv_codes = pair.tile([P, 1024], U32, tag="wv_codes%d" % gp, align_bytes=64)
             wv_scales = pair.tile([P, 1024], U8, tag="wv_scales%d" % gp, align_bytes=64)
             wv_q[(s, gp)] = (wv_codes, wv_scales)
-            return transpose_round(wv_sb[s], 512, four_tiles(4 * gp), wv_codes, wv_scales, engines, late)
+            return transpose_round(src, step, 512, four_tiles, wv_codes, wv_scales, engines, late)
 
-        def w1_round(s, engines, late):
+        def w1_round(s, src, step, engines, late):
             w1_codes = pair.tile([P, 1024], U32, tag="w1_codes", align_bytes=64)
             w1_scales = pair.tile([P, 1024], U8, tag="w1_scales", align_bytes=64)
             w1_q[s] = (w1_codes, w1_scales)
             banks = [(n, 0, n) for n in range(4)]
-            return transpose_round(w1_sb[s], 1024, banks, w1_codes, w1_scales, engines, late)
+            return transpose_round(src, step, 1024, banks, w1_codes, w1_scales, engines, late)
 
         def views_round(s, gp, engines, late, fine):
             wv_codes, wv_scales = wv_q[(s, gp)]
@@ -208,21 +223,27 @@ def tile_distributedb_pa_kernel(tc, x, h, Wv, W1, out):
             return None
 
         T_ENG = "VSSS"
-        V_ENG = "VSVS"
-        flush(transpose_round(h_sb, 512, four_tiles(0), h_codes, h_scales, "VSVS", None))
-        flush(wv_round(0, 0, "VSVS", None))
-        late = wv_round(0, 1, "VSVS", None)
-        late = views_round(0, 0, V_ENG, late, False)
-        late = views_round(0, 1, V_ENG, late, False)
-        late = w1_round(0, T_ENG, late)
-        late = transpose_round(x_sb, 512, four_tiles(0), x_codes, x_scales, T_ENG, late)
+        V_ENG = "SSSS"
+        flush(transpose_round(h_sb[:], 2, 512, four_tiles, h_codes, h_scales, "VSVS", None))
+        flush(wv_round(0, 0, wv_source(0, 0), 2, "VSVS", None))
+        late = wv_round(0, 1, wv_source(0, 1), 2, "VSVS", None)
+        late = views_round(0, 0, "VSVS", late, False)
+        w1_next = reorder(w1_sb[0][:])
+        late = views_round(0, 1, "VSSS", late, False)
+        x_next = reorder(x_sb[:])
+        late = w1_round(0, w1_next[:], 1, T_ENG, late)
+        wv_next = reorder(wv_source(1, 0))
+        late = transpose_round(x_next[:], 1, 512, four_tiles, x_codes, x_scales, T_ENG, late)
         for s in range(1, NS):
             if s > 1:
-                late = w1_round(s - 1, T_ENG, late)
-            late = wv_round(s, 0, T_ENG, late)
-            late = wv_round(s, 1, T_ENG, late)
+                wv_next = reorder(wv_source(s, 0))
+                late = w1_round(s - 1, w1_next[:], 1, T_ENG, late)
+            wv_after = reorder(wv_source(s, 1))
+            late = wv_round(s, 0, wv_next[:], 1, T_ENG, late)
+            w1_next = reorder(w1_sb[s][:])
+            late = wv_round(s, 1, wv_after[:], 1, T_ENG, late)
             if s == NS - 1:
-                late = w1_round(s, T_ENG, late)
+                late = w1_round(s, w1_next[:], 1, T_ENG, late)
             late = out_round(s - 1, late, False)
             late = views_round(s, 0, V_ENG, late, False)
             if s < NS - 1:

@@ -24,17 +24,18 @@ def tile_distributedb_pa_kernel(tc, x, h, Wv, W1, out):
     with ExitStack() as ctx:
         const = ctx.enter_context(tc.tile_pool(name="const", bufs=1))
         inputs = ctx.enter_context(tc.tile_pool(name="inputs", bufs=1))
+        raw = ctx.enter_context(tc.tile_pool(name="raw", bufs=3))
         stage = ctx.enter_context(tc.tile_pool(name="stage", bufs=3))
         keep = ctx.enter_context(tc.tile_pool(name="keep", bufs=1))
-        ordered = ctx.enter_context(tc.tile_pool(name="ordered", bufs=2))
+        ordered = ctx.enter_context(tc.tile_pool(name="ordered", bufs=3))
         pair = ctx.enter_context(tc.tile_pool(name="pair", bufs=2))
         psum = ctx.enter_context(tc.psum_pool(name="psum", bufs=8))
         ctx.enter_context(tc.manual_schedule())
 
         h_sb = inputs.tile([P, 4 * D], BF16, name="h_sb")
         x_sb = inputs.tile([P, 4 * D], BF16, name="x_sb")
-        wv_sb = [inputs.tile([P, 8 * D], BF16, name="wv_sb%d" % s) for s in range(NS)]
-        w1_sb = [inputs.tile([P, 2 * (D + DV)], BF16, name="w1_sb%d" % s) for s in range(NS)]
+        wv_sb = []
+        w1_sb = []
 
         def load_rows(dst, src):
             view = src.flatten_outer_dims().rearrange("(m j) d -> m (j d)", j=4)
@@ -58,15 +59,20 @@ def tile_distributedb_pa_kernel(tc, x, h, Wv, W1, out):
                 in_=W1[s].rearrange("(a m) k -> m a k", a=2),
             )
 
-        load_rows(h_sb, h)
-        load_wv(0, 0)
-        load_wv(0, 1)
-        load_w1(0)
-        load_rows(x_sb, x)
-        for s in range(1, NS):
+        def load_subnet(s):
+            wv_tile = raw.tile([P, 8 * D], BF16, tag="wv_sb")
+            w1_tile = raw.tile([P, 2 * (D + DV)], BF16, tag="w1_sb")
+            wv_sb.append(wv_tile)
+            w1_sb.append(w1_tile)
             load_wv(s, 0)
             load_wv(s, 1)
             load_w1(s)
+
+        load_rows(h_sb, h)
+        load_subnet(0)
+        load_rows(x_sb, x)
+        load_subnet(1)
+        load_subnet(2)
 
         ident = const.tile([P, P], F32, name="ident")
         make_identity(nc, ident[:])
@@ -81,21 +87,22 @@ def tile_distributedb_pa_kernel(tc, x, h, Wv, W1, out):
             else:
                 nc.scalar.copy(out=dst, in_=src)
 
-        def flush(late):
-            if late is not None:
-                late()
+        def do(jobs, n):
+            for job in jobs.get(n, []):
+                job()
 
-        def reorder(src):
+        def reorder(key, src):
             dst = ordered.tile([P, 4096], BF16, tag="dst", align_bytes=64)
+            ready[key] = dst
             nc.vector.tensor_copy(
                 out=dst[:].bitcast(F32).rearrange("p (b u w) -> p b u w", u=2, w=128),
                 in_=src.bitcast(F32).rearrange("p (b w u) -> p b u w", u=2, w=128),
             )
-            return dst
 
-        def transpose_round(src, step, tile_words, banks, codes, scales, engines, late):
+        def transpose_round(src, step, tile_words, banks, key, engines, jobs):
             words = src.bitcast(F32)
             grouped = stage.tile([P, 4096], BF16, tag="grouped", align_bytes=64)
+            grouped_of[key] = grouped
             grouped_words = grouped[:].bitcast(F32)
             for n, (slot, first_tile, k_pass) in enumerate(banks):
                 bank = psum.tile([P, 512], F32, tag="bank")
@@ -113,141 +120,159 @@ def tile_distributedb_pa_kernel(tc, x, h, Wv, W1, out):
                     grouped_words[:, 512 * slot : 512 * (slot + 1)].rearrange("p (c u) -> p c u", u=2),
                     bank[:].rearrange("p (u c) -> p c u", u=2),
                 )
-                if n == 0:
-                    flush(late)
-            return lambda: nc.vector.quantize_mx(
-                out=codes[:].bitcast(FP8X4), scales=scales[:], in_=grouped[:]
-            )
+                do(jobs, n)
+
+        def quantise(key):
+            if key[0] == "wv":
+                codes = pair.tile([P, 1024], U32, tag="wv_codes%d" % key[2], align_bytes=64)
+                scales = pair.tile([P, 1024], U8, tag="wv_scales%d" % key[2], align_bytes=64)
+            elif key[0] == "w1":
+                codes = pair.tile([P, 1024], U32, tag="w1_codes", align_bytes=64)
+                scales = pair.tile([P, 1024], U8, tag="w1_scales", align_bytes=64)
+            else:
+                codes = keep.tile([P, 1024], U32, tag="%s_codes" % key[0], align_bytes=64)
+                scales = keep.tile([P, 1024], U8, tag="%s_scales" % key[0], align_bytes=64)
+            quantised[key] = (codes, scales)
+            nc.vector.quantize_mx(out=codes[:].bitcast(FP8X4), scales=scales[:], in_=grouped_of[key][:])
 
         four_tiles = [(0, 0, 0), (2, 0, 1), (1, 2, 0), (3, 2, 1)]
+        two_tiles = [(n, 0, n) for n in range(4)]
 
-        h_codes = keep.tile([P, 1024], U32, name="h_codes", align_bytes=64)
-        h_scales = keep.tile([P, 1024], U8, name="h_scales", align_bytes=64)
-        x_codes = keep.tile([P, 1024], U32, name="x_codes", align_bytes=64)
-        x_scales = keep.tile([P, 1024], U8, name="x_scales", align_bytes=64)
-        wv_q = {}
-        w1_q = {}
+        ready = {}
+        grouped_of = {}
+        quantised = {}
+        views_grouped = {}
         views_q = {}
 
-        def wv_source(s, gp):
-            return wv_sb[s][:, 4 * D * gp : 4 * D * (gp + 1)]
+        def raw_of(key):
+            if key[0] == "h":
+                return h_sb[:]
+            if key[0] == "x":
+                return x_sb[:]
+            if key[0] == "w1":
+                return w1_sb[key[1]][:]
+            return wv_sb[key[1]][:, 4 * D * key[2] : 4 * D * (key[2] + 1)]
 
-        def wv_round(s, gp, src, step, engines, late):
-            wv_codes = pair.tile([P, 1024], U32, tag="wv_codes%d" % gp, align_bytes=64)
-            wv_scales = pair.tile([P, 1024], U8, tag="wv_scales%d" % gp, align_bytes=64)
-            wv_q[(s, gp)] = (wv_codes, wv_scales)
-            return transpose_round(src, step, 512, four_tiles, wv_codes, wv_scales, engines, late)
+        def T(key, engines, jobs):
+            src, step = (ready[key][:], 1) if key in ready else (raw_of(key), 2)
+            tile_words, banks = (1024, two_tiles) if key[0] == "w1" else (512, four_tiles)
+            transpose_round(src, step, tile_words, banks, key, engines, jobs)
 
-        def w1_round(s, src, step, engines, late):
-            w1_codes = pair.tile([P, 1024], U32, tag="w1_codes", align_bytes=64)
-            w1_scales = pair.tile([P, 1024], U8, tag="w1_scales", align_bytes=64)
-            w1_q[s] = (w1_codes, w1_scales)
-            banks = [(n, 0, n) for n in range(4)]
-            return transpose_round(src, step, 1024, banks, w1_codes, w1_scales, engines, late)
+        def perm(key):
+            return lambda: reorder(key, raw_of(key))
 
-        def views_round(s, gp, engines, late, fine):
-            wv_codes, wv_scales = wv_q[(s, gp)]
+        def quant(key):
+            return lambda: quantise(key)
+
+        def quantise_views(s, gp, j0, j1):
+            v_codes, v_scales = views_q[(s, gp)]
+            nc.vector.quantize_mx(
+                out=v_codes[:, 128 * j0 : 128 * j1].bitcast(FP8X4),
+                scales=v_scales[:, 128 * j0 : 128 * j1],
+                in_=views_grouped[(s, gp)][:, 512 * j0 : 512 * j1],
+            )
+
+        def quant_views(s, gp, j0=0, j1=4):
+            return lambda: quantise_views(s, gp, j0, j1)
+
+        def views_tile(s, gp):
             v_grouped = pair.tile([P, 2048], BF16, tag="v_grouped%d" % gp, align_bytes=64)
             v_codes = pair.tile([P, 512], U32, tag="v_codes%d" % gp, align_bytes=64)
             v_scales = pair.tile([P, 512], U8, tag="v_scales%d" % gp, align_bytes=64)
+            views_grouped[(s, gp)] = v_grouped
             views_q[(s, gp)] = (v_codes, v_scales)
 
-            def quantise(j0, j1):
-                nc.vector.quantize_mx(
-                    out=v_codes[:, 128 * j0 : 128 * j1].bitcast(FP8X4),
-                    scales=v_scales[:, 128 * j0 : 128 * j1],
-                    in_=v_grouped[:, 512 * j0 : 512 * j1],
-                )
-
-            for j in range(4):
-                bank = psum.tile([P, 512], F32, tag="bank")
-                for t in range(4):
-                    for g in range(2):
-                        wc = slice(512 * g + 128 * t, 512 * g + 128 * (t + 1))
-                        hc = slice(512 * g + 128 * j, 512 * g + 128 * (j + 1))
-                        nc.tensor.matmul_mx(
-                            out=bank[:, 128 * t : 128 * (t + 1)],
-                            lhsT=wv_codes[:, wc].bitcast(FP8X4),
-                            lhsT_scale=wv_scales[:, wc],
-                            rhs=h_codes[:, hc].bitcast(FP8X4),
-                            rhs_scale=h_scales[:, hc],
-                            start=(g == 0),
-                            stop=(g == 1),
-                        )
-                copy_out(
-                    engines[j],
-                    v_grouped[:, 512 * j : 512 * (j + 1)].rearrange("p (c t) -> p c t", t=4),
-                    bank[:].rearrange("p (t c) -> p c t", t=4),
-                )
-                if j == 0:
-                    flush(late)
-                if fine and j > 0:
-                    quantise(j - 1, j)
-            if fine:
-                quantise(3, 4)
-                return None
-            return lambda: quantise(0, 4)
-
-        def out_round(s, late, fine):
-            w1_codes, w1_scales = w1_q[s]
-            o_sb = pair.tile([P, 4 * SD], F32, tag="o_sb")
-            o_view = out[s].rearrange("b q f -> (b q) f").rearrange("(m j) f -> m (j f)", j=4)
-            bank = None
-            for j in range(4):
-                if fine or j % 2 == 0:
-                    bank = psum.tile([P, 512], F32, tag="bank")
-                c0 = 0 if fine else 256 * (j % 2)
-                operands = [(x_codes, x_scales, 512 * g + 128 * j) for g in range(2)]
-                operands.extend([views_q[(s, gp)] + (128 * j,) for gp in range(2)])
-                for n, (codes, scales, col) in enumerate(operands):
+        def views_bank(s, gp, j, engine):
+            wv_codes, wv_scales = quantised[("wv", s, gp)]
+            h_codes, h_scales = quantised[("h",)]
+            v_grouped = views_grouped[(s, gp)]
+            bank = psum.tile([P, 512], F32, tag="bank")
+            for t in range(4):
+                for g in range(2):
+                    wc = slice(512 * g + 128 * t, 512 * g + 128 * (t + 1))
+                    hc = slice(512 * g + 128 * j, 512 * g + 128 * (j + 1))
                     nc.tensor.matmul_mx(
-                        out=bank[:, c0 : c0 + 256],
-                        lhsT=codes[:, col : col + 128].bitcast(FP8X4),
-                        lhsT_scale=scales[:, col : col + 128],
-                        rhs=w1_codes[:, 256 * n : 256 * (n + 1)].bitcast(FP8X4),
-                        rhs_scale=w1_scales[:, 256 * n : 256 * (n + 1)],
-                        start=(n == 0),
-                        stop=(n == 3),
+                        out=bank[:, 128 * t : 128 * (t + 1)],
+                        lhsT=wv_codes[:, wc].bitcast(FP8X4),
+                        lhsT_scale=wv_scales[:, wc],
+                        rhs=h_codes[:, hc].bitcast(FP8X4),
+                        rhs_scale=h_scales[:, hc],
+                        start=(g == 0),
+                        stop=(g == 1),
                     )
-                if fine:
-                    cols = slice(256 * j, 256 * (j + 1))
-                    nc.scalar.activation(out=o_sb[:, cols], in_=bank[:, 0:256], func=SILU)
-                    nc.sync.dma_start(out=o_view[:, cols], in_=o_sb[:, cols])
-                elif j % 2 == 1:
-                    cols = slice(256 * (j - 1), 256 * (j + 1))
-                    nc.scalar.activation(out=o_sb[:, cols], in_=bank[:], func=SILU)
-                if j == 1:
-                    flush(late)
-            if not fine:
-                nc.sync.dma_start(out=o_view, in_=o_sb[:])
-            return None
+            copy_out(
+                engine,
+                v_grouped[:, 512 * j : 512 * (j + 1)].rearrange("p (c t) -> p c t", t=4),
+                bank[:].rearrange("p (t c) -> p c t", t=4),
+            )
 
-        T_ENG = "VSSS"
-        V_ENG = "SSSS"
-        flush(transpose_round(h_sb[:], 2, 512, four_tiles, h_codes, h_scales, "VSVS", None))
-        flush(wv_round(0, 0, wv_source(0, 0), 2, "VSVS", None))
-        late = wv_round(0, 1, wv_source(0, 1), 2, "VSVS", None)
-        late = views_round(0, 0, "VSVS", late, False)
-        w1_next = reorder(w1_sb[0][:])
-        late = views_round(0, 1, "VSSS", late, False)
-        x_next = reorder(x_sb[:])
-        late = w1_round(0, w1_next[:], 1, T_ENG, late)
-        wv_next = reorder(wv_source(1, 0))
-        late = transpose_round(x_next[:], 1, 512, four_tiles, x_codes, x_scales, T_ENG, late)
+        def V(s, gp, engines, jobs):
+            views_tile(s, gp)
+            for j in range(4):
+                views_bank(s, gp, j, engines[j])
+                do(jobs, j)
+
+        def out_view(s):
+            return out[s].rearrange("b q f -> (b q) f").rearrange("(m j) f -> m (j f)", j=4)
+
+        def out_passes(s, j, dst):
+            w1_codes, w1_scales = quantised[("w1", s)]
+            x_codes, x_scales = quantised[("x",)]
+            operands = [(x_codes, x_scales, 512 * g + 128 * j) for g in range(2)]
+            operands.extend([views_q[(s, gp)] + (128 * j,) for gp in range(2)])
+            for n, (codes, scales, col) in enumerate(operands):
+                nc.tensor.matmul_mx(
+                    out=dst,
+                    lhsT=codes[:, col : col + 128].bitcast(FP8X4),
+                    lhsT_scale=scales[:, col : col + 128],
+                    rhs=w1_codes[:, 256 * n : 256 * (n + 1)].bitcast(FP8X4),
+                    rhs_scale=w1_scales[:, 256 * n : 256 * (n + 1)],
+                    start=(n == 0),
+                    stop=(n == 3),
+                )
+
+        def O(s, jobs):
+            o_sb = pair.tile([P, 4 * SD], F32, tag="o_sb")
+            for half in range(2):
+                bank = psum.tile([P, 512], F32, tag="bank")
+                for e in range(2):
+                    out_passes(s, 2 * half + e, bank[:, 256 * e : 256 * (e + 1)])
+                cols = slice(512 * half, 512 * (half + 1))
+                nc.scalar.activation(out=o_sb[:, cols], in_=bank[:], func=SILU)
+                do(jobs, half)
+            nc.sync.dma_start(out=out_view(s), in_=o_sb[:])
+
+        def O_fine(s, j, o_sb):
+            bank = psum.tile([P, 512], F32, tag="bank")
+            out_passes(s, j, bank[:, 0:256])
+            cols = slice(256 * j, 256 * (j + 1))
+            nc.scalar.activation(out=o_sb[:, cols], in_=bank[:, 0:256], func=SILU)
+            nc.sync.dma_start(out=out_view(s)[:, cols], in_=o_sb[:, cols])
+
+        H, X = ("h",), ("x",)
+        T(H, "VSVS", {})
+        T(("wv", 0, 0), "VSVS", {0: [quant(H)]})
+        T(("wv", 0, 1), "SVSV", {0: [quant(("wv", 0, 0))], 3: [perm(("w1", 0))]})
+        V(0, 0, "SSSS", {0: [quant(("wv", 0, 1))], 2: [perm(X)]})
+        T(("w1", 0), "SVSV", {1: [quant_views(0, 0)]})
+        T(X, "SVSV", {0: [quant(("w1", 0)), perm(("wv", 1, 0))]})
+        V(0, 1, "SSSS", {0: [quant(X)], 2: [perm(("wv", 1, 1))]})
+        load_subnet(3)
+        T(("wv", 1, 0), "SVSV", {0: [quant_views(0, 1)]})
+        O(0, {0: [quant(("wv", 1, 0)), perm(("w1", 1))]})
+        T(("wv", 1, 1), "SSSV", {})
+        T(("w1", 1), "SSSV", {0: [quant(("wv", 1, 1))]})
         for s in range(1, NS):
             if s > 1:
-                wv_next = reorder(wv_source(s, 0))
-                late = w1_round(s - 1, w1_next[:], 1, T_ENG, late)
-            wv_after = reorder(wv_source(s, 1))
-            late = wv_round(s, 0, wv_next[:], 1, T_ENG, late)
-            w1_next = reorder(w1_sb[s][:])
-            late = wv_round(s, 1, wv_after[:], 1, T_ENG, late)
-            if s == NS - 1:
-                late = w1_round(s, w1_next[:], 1, T_ENG, late)
-            late = out_round(s - 1, late, False)
-            late = views_round(s, 0, V_ENG, late, False)
+                O(s - 1, {0: [quant(("wv", s, 1))]})
+                T(("w1", s), "SSSS", {})
+            V(s, 0, "SSSS", {0: [quant(("w1", s))], 1: [perm(("wv", s + 1, 0))] if s < NS - 1 else []})
             if s < NS - 1:
-                late = views_round(s, 1, V_ENG, late, False)
-            else:
-                views_round(s, 1, "SSSV", late, True)
-        out_round(NS - 1, None, True)
+                V(s, 1, "SSSS", {0: [quant_views(s, 0)], 1: [perm(("wv", s + 1, 1))]})
+                T(("wv", s + 1, 0), "VSVS", {0: [quant_views(s, 1)], 1: [perm(("w1", s + 1))]})
+                T(("wv", s + 1, 1), "VSVS", {0: [quant(("wv", s + 1, 0))]})
+        s = NS - 1
+        o_sb = pair.tile([P, 4 * SD], F32, tag="o_sb")
+        V(s, 1, "SSSV", {0: [quant_views(s, 0)], 1: [quant_views(s, 1, 0, 1)], 2: [quant_views(s, 1, 1, 2)], 3: [quant_views(s, 1, 2, 3), quant_views(s, 1, 3, 4)]})
+        for j in range(4):
+            O_fine(s, j, o_sb)

@@ -54,10 +54,11 @@ def tile_distributedb_pa_kernel(tc, x, h, Wv, W1, out):
                 )
 
         def load_w1(s):
-            nc.sync.dma_start(
-                out=w1_sb[s][:].rearrange("m (a k) -> m a k", a=2),
-                in_=W1[s].rearrange("(a m) k -> m a k", a=2),
-            )
+            for half in range(2):
+                nc.sync.dma_start(
+                    out=w1_sb[s][:, 2 * D * half : 2 * D * (half + 1)].rearrange("m (a k) -> m a k", a=2),
+                    in_=W1[s].rearrange("(a m) k -> m a k", a=2)[:, :, D * half : D * (half + 1)],
+                )
 
         def load_subnet(s):
             wv_tile = raw.tile([P, 8 * D], BF16, tag="wv_sb")
@@ -136,7 +137,7 @@ def tile_distributedb_pa_kernel(tc, x, h, Wv, W1, out):
             nc.vector.quantize_mx(out=codes[:].bitcast(FP8X4), scales=scales[:], in_=grouped_of[key][:])
 
         four_tiles = [(0, 0, 0), (2, 0, 1), (1, 2, 0), (3, 2, 1)]
-        two_tiles = [(n, 0, n) for n in range(4)]
+        two_tiles = [(0, 0, 0), (1, 0, 1), (2, 2, 0), (3, 2, 1)]
 
         ready = {}
         grouped_of = {}
@@ -155,7 +156,7 @@ def tile_distributedb_pa_kernel(tc, x, h, Wv, W1, out):
 
         def T(key, engines, jobs):
             src, step = (ready[key][:], 1) if key in ready else (raw_of(key), 2)
-            tile_words, banks = (1024, two_tiles) if key[0] == "w1" else (512, four_tiles)
+            tile_words, banks = 512, two_tiles if key[0] == "w1" else four_tiles
             transpose_round(src, step, tile_words, banks, key, engines, jobs)
 
         def perm(key):
@@ -250,18 +251,21 @@ def tile_distributedb_pa_kernel(tc, x, h, Wv, W1, out):
             nc.sync.dma_start(out=out_view(s)[:, cols], in_=o_sb[:, cols])
 
         H, X = ("h",), ("x",)
-        T(H, "VSVS", {})
-        T(("wv", 0, 0), "VSVS", {0: [quant(H)]})
-        T(("wv", 0, 1), "SVSV", {0: [quant(("wv", 0, 0))], 3: [perm(("w1", 0))]})
-        V(0, 0, "SSSS", {0: [quant(("wv", 0, 1))], 2: [perm(X)]})
-        T(("w1", 0), "SVSV", {1: [quant_views(0, 0)]})
-        T(X, "SVSV", {0: [quant(("w1", 0)), perm(("wv", 1, 0))]})
-        V(0, 1, "SSSS", {0: [quant(X)], 2: [perm(("wv", 1, 1))]})
+        W00, W01, W10, W11 = [("wv", s, gp) for s in range(2) for gp in range(2)]
+        A0, A1 = ("w1", 0), ("w1", 1)
+        T(H, "VSSS", {})
+        T(W00, "VSSS", {0: [quant(H)]})
+        T(W01, "SSSS", {0: [quant(W00)]})
+        perm(A0)()
+        V(0, 0, "SSSS", {0: [quant(W01)], 1: [perm(X)]})
+        T(A0, "SSSS", {})
+        V(0, 1, "SSSS", {0: [quant_views(0, 0), quant(A0)], 1: [perm(W10)]})
+        T(X, "SSSS", {0: [perm(W11)], 2: [quant_views(0, 1)]})
         load_subnet(3)
-        T(("wv", 1, 0), "SVSV", {0: [quant_views(0, 1)]})
-        O(0, {0: [quant(("wv", 1, 0)), perm(("w1", 1))]})
-        T(("wv", 1, 1), "SSSV", {})
-        T(("w1", 1), "SSSV", {0: [quant(("wv", 1, 1))]})
+        T(W10, "SVSV", {2: [quant(X)]})
+        T(W11, "SSSS", {0: [perm(A1)]})
+        O(0, {0: [quant(W10)]})
+        T(A1, "SVSV", {1: [quant(W11)]})
         for s in range(1, NS):
             if s > 1:
                 O(s - 1, {0: [quant(("wv", s, 1))]})

@@ -37,21 +37,14 @@ def tile_distributedb_pa_kernel(tc, x, h, Wv, W1, out):
         wv_sb = []
         w1_sb = []
 
-        def load_rows(dst, src):
-            view = src.flatten_outer_dims().rearrange("(m j) d -> m (j d)", j=4)
-            for half in range(2):
-                cols = slice(2 * D * half, 2 * D * (half + 1))
+        def load_rows(dst, src, pieces):
+            view = src.rearrange("(m j) d -> m (j d)", j=4)
+            for i in range(pieces):
+                cols = slice(4 * D * i // pieces, 4 * D * (i + 1) // pieces)
                 nc.sync.dma_start(out=dst[:, cols], in_=view[:, cols])
 
-        def load_wv(s, gp):
-            for u in range(2):
-                tile0 = 4 * gp + 2 * u
-                nc.sync.dma_start(
-                    out=wv_sb[s][:, tile0 * D : (tile0 + 2) * D],
-                    in_=Wv[s, 512 * gp : 512 * (gp + 1), :].rearrange("(m t) d -> m (t d)", t=4)[
-                        :, 2 * D * u : 2 * D * (u + 1)
-                    ],
-                )
+        def load_wv(s, gp, pieces):
+            load_rows(wv_sb[s][:, 4 * D * gp : 4 * D * (gp + 1)], Wv[s, 512 * gp : 512 * (gp + 1), :], pieces)
 
         def load_w1(s):
             for half in range(2):
@@ -60,20 +53,20 @@ def tile_distributedb_pa_kernel(tc, x, h, Wv, W1, out):
                     in_=W1[s].rearrange("(a m) k -> m a k", a=2)[:, :, D * half : D * (half + 1)],
                 )
 
-        def load_subnet(s):
+        def load_subnet(s, pieces):
             wv_tile = raw.tile([P, 8 * D], BF16, tag="wv_sb")
             w1_tile = raw.tile([P, 2 * (D + DV)], BF16, tag="w1_sb")
             wv_sb.append(wv_tile)
             w1_sb.append(w1_tile)
-            load_wv(s, 0)
-            load_wv(s, 1)
+            load_wv(s, 0, pieces)
+            load_wv(s, 1, pieces)
             load_w1(s)
 
-        load_rows(h_sb, h)
-        load_subnet(0)
-        load_rows(x_sb, x)
-        load_subnet(1)
-        load_subnet(2)
+        load_rows(h_sb, h.flatten_outer_dims(), 4)
+        load_subnet(0, 4)
+        load_rows(x_sb, x.flatten_outer_dims(), 2)
+        load_subnet(1, 2)
+        load_subnet(2, 2)
 
         ident = const.tile([P, P], F32, name="ident")
         make_identity(nc, ident[:])
@@ -92,39 +85,58 @@ def tile_distributedb_pa_kernel(tc, x, h, Wv, W1, out):
             for job in jobs.get(n, []):
                 job()
 
-        def reorder(key, src):
-            dst = ordered.tile([P, 4096], BF16, tag="dst", align_bytes=64)
-            ready[key] = dst
-            nc.vector.tensor_copy(
-                out=dst[:].bitcast(F32).rearrange("p (b u w) -> p b u w", u=2, w=128),
-                in_=src.bitcast(F32).rearrange("p (b w u) -> p b u w", u=2, w=128),
-            )
+        def reorder(key, halves):
+            if key not in ready:
+                ready[key] = ordered.tile([P, 4096], BF16, tag="dst", align_bytes=64, name="dst")
+            by_eight = [key[0] == "x", key[0] == "x"] if key[0] != "w1" else [True, False]
+            for half in halves:
+                cols = slice(2048 * half, 2048 * (half + 1))
+                dst, src = ready[key][:, cols], raw_of(key)[:, cols]
+                if by_eight[half]:
+                    nc.vector.tensor_copy(
+                        out=dst.rearrange("p (u g r) -> p u g r", u=2, r=16),
+                        in_=src.rearrange("p (g u r) -> p u g r", u=2, r=16),
+                    )
+                else:
+                    nc.vector.tensor_copy(
+                        out=dst.bitcast(F32).rearrange("p (u w) -> p u w", u=2),
+                        in_=src.bitcast(F32).rearrange("p (w u) -> p u w", u=2),
+                    )
 
-        def transpose_round(src, step, tile_words, banks, key, engines, jobs):
+        def transpose_half(src, step, half, key, engines, jobs):
             words = src.bitcast(F32)
-            grouped = stage.tile([P, 4096], BF16, tag="grouped", align_bytes=64)
-            grouped_of[key] = grouped
-            grouped_words = grouped[:].bitcast(F32)
-            for n, (slot, first_tile, k_pass) in enumerate(banks):
-                bank = psum.tile([P, 512], F32, tag="bank")
-                for u in range(2):
-                    for i in range(2):
-                        w0 = (first_tile + i) * tile_words + 256 * k_pass
-                        c0 = 256 * u + 128 * i
-                        if step == 2:
-                            cols = slice(w0 + u, w0 + 256, 2)
-                        else:
-                            cols = slice(w0 + 128 * u, w0 + 128 * (u + 1))
-                        nc.tensor.transpose(bank[:, c0 : c0 + 128], words[:, cols], ident[:])
-                copy_out(
-                    engines[n],
-                    grouped_words[:, 512 * slot : 512 * (slot + 1)].rearrange("p (c u) -> p c u", u=2),
-                    bank[:].rearrange("p (u c) -> p c u", u=2),
-                )
-                do(jobs, n)
+            if half == 0:
+                grouped_of[key] = stage.tile([P, 4096], BF16, tag="grouped", align_bytes=64, name="grouped")
+            grouped_words = grouped_of[key][:].bitcast(F32)
+            banks = [psum.tile([P, 512], F32, tag="bank", name="bank") for g in range(2)]
+            order = [(i, g) for i in range(2) for g in range(2)] if step == 2 else [(i, g) for g in range(2) for i in range(2)]
 
-        def quantise(key):
-            if key[0] == "wv":
+            def empty(g):
+                slot = 2 * half + g if key[0] == "w1" else half + 2 * g
+                copy_out(
+                    engines[2 * half + g],
+                    grouped_words[:, 512 * slot : 512 * (slot + 1)].rearrange("p (c u) -> p c u", u=2),
+                    banks[g][:].rearrange("p (u c) -> p c u", u=2),
+                )
+                do(jobs, 2 * half + g)
+
+            for i, g in order:
+                for u in range(2):
+                    c0 = 256 * u + 128 * i
+                    if step == 2:
+                        w0 = 1024 * half + 512 * i + 256 * g
+                        cols = slice(w0 + u, w0 + 256, 2)
+                    else:
+                        w0 = 1024 * half + 512 * u + 256 * i + 128 * g
+                        cols = slice(w0, w0 + 128)
+                    nc.tensor.transpose(banks[g][:, c0 : c0 + 128], words[:, cols], ident[:])
+                if i == 1:
+                    empty(g)
+
+        def quantise(key, slots):
+            if key in quantised:
+                codes, scales = quantised[key]
+            elif key[0] == "wv":
                 codes = pair.tile([P, 1024], U32, tag="wv_codes%d" % key[2], align_bytes=64)
                 scales = pair.tile([P, 1024], U8, tag="wv_scales%d" % key[2], align_bytes=64)
             elif key[0] == "w1":
@@ -134,10 +146,11 @@ def tile_distributedb_pa_kernel(tc, x, h, Wv, W1, out):
                 codes = keep.tile([P, 1024], U32, tag="%s_codes" % key[0], align_bytes=64)
                 scales = keep.tile([P, 1024], U8, tag="%s_scales" % key[0], align_bytes=64)
             quantised[key] = (codes, scales)
-            nc.vector.quantize_mx(out=codes[:].bitcast(FP8X4), scales=scales[:], in_=grouped_of[key][:])
-
-        four_tiles = [(0, 0, 0), (2, 0, 1), (1, 2, 0), (3, 2, 1)]
-        two_tiles = [(0, 0, 0), (1, 0, 1), (2, 2, 0), (3, 2, 1)]
+            for slot in [None] if slots is None else slots:
+                cols, values = (slice(0, 1024), slice(0, 4096)) if slot is None else (slice(256 * slot, 256 * (slot + 1)), slice(1024 * slot, 1024 * (slot + 1)))
+                nc.vector.quantize_mx(
+                    out=codes[:, cols].bitcast(FP8X4), scales=scales[:, cols], in_=grouped_of[key][:, values]
+                )
 
         ready = {}
         grouped_of = {}
@@ -154,16 +167,16 @@ def tile_distributedb_pa_kernel(tc, x, h, Wv, W1, out):
                 return w1_sb[key[1]][:]
             return wv_sb[key[1]][:, 4 * D * key[2] : 4 * D * (key[2] + 1)]
 
-        def T(key, engines, jobs):
+        def T(key, engines, jobs, halves=(0, 1)):
             src, step = (ready[key][:], 1) if key in ready else (raw_of(key), 2)
-            tile_words, banks = 512, two_tiles if key[0] == "w1" else four_tiles
-            transpose_round(src, step, tile_words, banks, key, engines, jobs)
+            for half in halves:
+                transpose_half(src, step, half, key, engines, jobs)
 
-        def perm(key):
-            return lambda: reorder(key, raw_of(key))
+        def perm(key, halves=(0, 1)):
+            return lambda: reorder(key, halves)
 
-        def quant(key):
-            return lambda: quantise(key)
+        def quant(key, slots=None):
+            return lambda: quantise(key, slots)
 
         def quantise_views(s, gp, j0, j1):
             v_codes, v_scales = views_q[(s, gp)]
@@ -256,13 +269,13 @@ def tile_distributedb_pa_kernel(tc, x, h, Wv, W1, out):
         T(H, "VSSS", {})
         T(W00, "VSSS", {0: [quant(H)]})
         T(W01, "SSSS", {0: [quant(W00)]})
-        perm(A0)()
-        V(0, 0, "SSSS", {0: [quant(W01)], 1: [perm(X)]})
+        perm(A0, [0])()
+        V(0, 0, "SSSS", {0: [quant(W01), perm(A0, [1])], 1: [perm(X)]})
         T(A0, "SSSS", {})
-        V(0, 1, "SSSS", {0: [quant_views(0, 0), quant(A0)], 1: [perm(W10)]})
-        T(X, "SSSS", {0: [perm(W11)], 2: [quant_views(0, 1)]})
-        load_subnet(3)
-        T(W10, "SVSV", {2: [quant(X)]})
+        V(0, 1, "SSSS", {0: [quant_views(0, 0), perm(W10), quant(A0)], 3: [perm(W11)]})
+        T(X, "SVSS", {3: [quant_views(0, 1)]})
+        load_subnet(3, 2)
+        T(W10, "SSSV", {0: [quant(X)]})
         T(W11, "SSSS", {0: [perm(A1)]})
         O(0, {0: [quant(W10)]})
         T(A1, "SVSV", {1: [quant(W11)]})
@@ -274,7 +287,7 @@ def tile_distributedb_pa_kernel(tc, x, h, Wv, W1, out):
             if s < NS - 1:
                 V(s, 1, "SSSS", {0: [quant_views(s, 0)], 1: [perm(("wv", s + 1, 1))]})
                 T(("wv", s + 1, 0), "VSVS", {0: [quant_views(s, 1)], 1: [perm(("w1", s + 1))]})
-                T(("wv", s + 1, 1), "VSVS", {0: [quant(("wv", s + 1, 0))]})
+                T(("wv", s + 1, 1), "VSSS", {0: [quant(("wv", s + 1, 0))]})
         s = NS - 1
         o_sb = pair.tile([P, 4 * SD], F32, tag="o_sb")
         V(s, 1, "SSSV", {0: [quant_views(s, 0)], 1: [quant_views(s, 1, 0, 1)], 2: [quant_views(s, 1, 1, 2)], 3: [quant_views(s, 1, 2, 3), quant_views(s, 1, 3, 4)]})

@@ -47,11 +47,7 @@ def tile_distributedb_pa_kernel(tc, x, h, Wv, W1, out):
             load_rows(wv_sb[s][:, 4 * D * gp : 4 * D * (gp + 1)], Wv[s, 512 * gp : 512 * (gp + 1), :], pieces)
 
         def load_w1(s):
-            for half in range(2):
-                nc.sync.dma_start(
-                    out=w1_sb[s][:, 2 * D * half : 2 * D * (half + 1)].rearrange("m (a k) -> m a k", a=2),
-                    in_=W1[s].rearrange("(a m) k -> m a k", a=2)[:, :, D * half : D * (half + 1)],
-                )
+            nc.sync.dma_start(out=w1_sb[s][:], in_=W1[s].rearrange("(m a) k -> m (a k)", a=2))
 
         def load_subnet(s, pieces):
             wv_tile = raw.tile([P, 8 * D], BF16, tag="wv_sb")
@@ -62,11 +58,11 @@ def tile_distributedb_pa_kernel(tc, x, h, Wv, W1, out):
             load_wv(s, 1, pieces)
             load_w1(s)
 
-        load_rows(h_sb, h.flatten_outer_dims(), 4)
-        load_subnet(0, 4)
-        load_rows(x_sb, x.flatten_outer_dims(), 2)
-        load_subnet(1, 2)
-        load_subnet(2, 2)
+        load_rows(h_sb, h.flatten_outer_dims(), 2)
+        load_subnet(0, 2)
+        load_rows(x_sb, x.flatten_outer_dims(), 1)
+        load_subnet(1, 1)
+        load_subnet(2, 1)
 
         ident = const.tile([P, P], F32, name="ident")
         make_identity(nc, ident[:])
@@ -88,20 +84,13 @@ def tile_distributedb_pa_kernel(tc, x, h, Wv, W1, out):
         def reorder(key, halves):
             if key not in ready:
                 ready[key] = ordered.tile([P, 4096], BF16, tag="dst", align_bytes=64, name="dst")
-            by_eight = [key[0] == "x", key[0] == "x"] if key[0] != "w1" else [True, False]
             for half in halves:
-                cols = slice(2048 * half, 2048 * (half + 1))
-                dst, src = ready[key][:, cols], raw_of(key)[:, cols]
-                if by_eight[half]:
-                    nc.vector.tensor_copy(
-                        out=dst.rearrange("p (u g r) -> p u g r", u=2, r=16),
-                        in_=src.rearrange("p (g u r) -> p u g r", u=2, r=16),
-                    )
-                else:
-                    nc.vector.tensor_copy(
-                        out=dst.bitcast(F32).rearrange("p (u w) -> p u w", u=2),
-                        in_=src.bitcast(F32).rearrange("p (w u) -> p u w", u=2),
-                    )
+                nc.vector.tensor_copy(
+                    out=ready[key][:, 2048 * half : 2048 * (half + 1)]
+                    .bitcast(F32)
+                    .rearrange("p (u i w) -> p u i w", u=2, i=2),
+                    in_=raw_half(key, half).bitcast(F32).rearrange("p i (w u) -> p u i w", u=2),
+                )
 
         def transpose_half(src, step, half, key, engines, jobs):
             words = src.bitcast(F32)
@@ -166,6 +155,11 @@ def tile_distributedb_pa_kernel(tc, x, h, Wv, W1, out):
             if key[0] == "w1":
                 return w1_sb[key[1]][:]
             return wv_sb[key[1]][:, 4 * D * key[2] : 4 * D * (key[2] + 1)]
+
+        def raw_half(key, half):
+            if key[0] == "w1":
+                return raw_of(key).rearrange("p (a k) -> p a k", a=2)[:, :, D * half : D * (half + 1)]
+            return raw_of(key)[:, 2 * D * half : 2 * D * (half + 1)].rearrange("p (i k) -> p i k", i=2)
 
         def T(key, engines, jobs, halves=(0, 1)):
             src, step = (ready[key][:], 1) if key in ready else (raw_of(key), 2)
@@ -252,7 +246,11 @@ def tile_distributedb_pa_kernel(tc, x, h, Wv, W1, out):
                 for e in range(2):
                     out_passes(s, 2 * half + e, bank[:, 256 * e : 256 * (e + 1)])
                 cols = slice(512 * half, 512 * (half + 1))
-                nc.scalar.activation(out=o_sb[:, cols], in_=bank[:], func=SILU)
+                nc.scalar.activation(
+                    out=o_sb[:, cols].rearrange("p (j m a) -> p j m a", j=2, a=2),
+                    in_=bank[:].rearrange("p (j a m) -> p j m a", j=2, a=2),
+                    func=SILU,
+                )
                 do(jobs, half)
             nc.sync.dma_start(out=out_view(s), in_=o_sb[:])
 
@@ -260,7 +258,11 @@ def tile_distributedb_pa_kernel(tc, x, h, Wv, W1, out):
             bank = psum.tile([P, 512], F32, tag="bank")
             out_passes(s, j, bank[:, 0:256])
             cols = slice(256 * j, 256 * (j + 1))
-            nc.scalar.activation(out=o_sb[:, cols], in_=bank[:, 0:256], func=SILU)
+            nc.scalar.activation(
+                out=o_sb[:, cols].rearrange("p (m a) -> p m a", a=2),
+                in_=bank[:, 0:256].rearrange("p (a m) -> p m a", a=2),
+                func=SILU,
+            )
             nc.sync.dma_start(out=out_view(s)[:, cols], in_=o_sb[:, cols])
 
         H, X = ("h",), ("x",)
@@ -274,7 +276,7 @@ def tile_distributedb_pa_kernel(tc, x, h, Wv, W1, out):
         T(A0, "SSSS", {})
         V(0, 1, "SSSS", {0: [quant_views(0, 0), perm(W10), quant(A0)], 3: [perm(W11)]})
         T(X, "SVSS", {3: [quant_views(0, 1)]})
-        load_subnet(3, 2)
+        load_subnet(3, 1)
         T(W10, "SSSV", {0: [quant(X)]})
         T(W11, "SSSS", {0: [perm(A1)]})
         O(0, {0: [quant(W10)]})

@@ -85,6 +85,7 @@ def tile_distributedb_pa_kernel(tc, x, h, Wv, W1, out):
             if key not in ready:
                 ready[key] = ordered.tile([P, 4096], BF16, tag="dst", align_bytes=64, name="dst")
             for half in halves:
+                reordered.add((key, half))
                 nc.vector.tensor_copy(
                     out=ready[key][:, 2048 * half : 2048 * (half + 1)]
                     .bitcast(F32)
@@ -113,7 +114,7 @@ def tile_distributedb_pa_kernel(tc, x, h, Wv, W1, out):
                 for u in range(2):
                     c0 = 256 * u + 128 * i
                     if step == 2:
-                        w0 = 1024 * half + 512 * i + 256 * g
+                        w0 = (512 * half + 1024 * i if key[0] == "w1" else 1024 * half + 512 * i) + 256 * g
                         cols = slice(w0 + u, w0 + 256, 2)
                     else:
                         w0 = 1024 * half + 512 * u + 256 * i + 128 * g
@@ -142,6 +143,7 @@ def tile_distributedb_pa_kernel(tc, x, h, Wv, W1, out):
                 )
 
         ready = {}
+        reordered = set()
         grouped_of = {}
         quantised = {}
         views_grouped = {}
@@ -162,8 +164,8 @@ def tile_distributedb_pa_kernel(tc, x, h, Wv, W1, out):
             return raw_of(key)[:, 2 * D * half : 2 * D * (half + 1)].rearrange("p (i k) -> p i k", i=2)
 
         def T(key, engines, jobs, halves=(0, 1)):
-            src, step = (ready[key][:], 1) if key in ready else (raw_of(key), 2)
             for half in halves:
+                src, step = (ready[key][:], 1) if (key, half) in reordered else (raw_of(key), 2)
                 transpose_half(src, step, half, key, engines, jobs)
 
         def perm(key, halves=(0, 1)):
@@ -271,8 +273,7 @@ def tile_distributedb_pa_kernel(tc, x, h, Wv, W1, out):
         T(H, "VSSS", {})
         T(W00, "VSSS", {0: [quant(H)]})
         T(W01, "SSSS", {0: [quant(W00)]})
-        perm(A0, [0])()
-        V(0, 0, "SSSS", {0: [quant(W01), perm(A0, [1])], 1: [perm(X)]})
+        V(0, 0, "SSSS", {0: [quant(W01)], 1: [perm(X)]})
         T(A0, "SSSS", {})
         V(0, 1, "SSSS", {0: [quant_views(0, 0), perm(W10), quant(A0)], 3: [perm(W11)]})
         T(X, "SVSS", {3: [quant_views(0, 1)]})
@@ -280,11 +281,11 @@ def tile_distributedb_pa_kernel(tc, x, h, Wv, W1, out):
         T(W10, "SSSV", {0: [quant(X)]})
         T(W11, "SSSS", {0: [perm(A1)]})
         O(0, {0: [quant(W10)]})
-        T(A1, "SVSV", {1: [quant(W11)]})
+        T(A1, "VSVS", {1: [quant(W11)]})
         for s in range(1, NS):
             if s > 1:
                 O(s - 1, {0: [quant(("wv", s, 1))]})
-                T(("w1", s), "SSSS", {})
+                T(("w1", s), "SSSV", {})
             V(s, 0, "SSSS", {0: [quant(("w1", s))], 1: [perm(("wv", s + 1, 0))] if s < NS - 1 else []})
             if s < NS - 1:
                 V(s, 1, "SSSS", {0: [quant_views(s, 0)], 1: [perm(("wv", s + 1, 1))]})

from contextlib import ExitStack

import concourse.mybir as mybir
from concourse.masks import make_identity

F32 = mybir.dt.float32
BF16 = mybir.dt.bfloat16
U32 = mybir.dt.uint32
U8 = mybir.dt.uint8
FP8X4 = mybir.dt.float8_e4m3fn_x4
SILU = mybir.ActivationFunctionType.Silu

P = 128
NS = 4
R = 512
D = 1024
DV = 1024
SD = 256
FLOPS = 2 * NS * R * (D * DV + (D + DV) * SD)


def tile_distributedb_pa_kernel(tc, x, h, Wv, W1, out):
    nc = tc.nc
    with ExitStack() as ctx:
        const = ctx.enter_context(tc.tile_pool(name="const", bufs=1))
        inputs = ctx.enter_context(tc.tile_pool(name="inputs", bufs=1))
        raw = ctx.enter_context(tc.tile_pool(name="raw", bufs=3))
        stage = ctx.enter_context(tc.tile_pool(name="stage", bufs=3))
        keep = ctx.enter_context(tc.tile_pool(name="keep", bufs=1))
        ordered = ctx.enter_context(tc.tile_pool(name="ordered", bufs=3))
        pair = ctx.enter_context(tc.tile_pool(name="pair", bufs=2))
        psum = ctx.enter_context(tc.psum_pool(name="psum", bufs=8))
        ctx.enter_context(tc.manual_schedule())

        h_sb = inputs.tile([P, 4 * D], BF16, name="h_sb")
        x_sb = inputs.tile([P, 4 * D], BF16, name="x_sb")
        wv_sb = []
        w1_sb = []

        def load_rows(dst, src, pieces):
            view = src.rearrange("(m j) d -> m (j d)", j=4)
            for i in range(pieces):
                cols = slice(4 * D * i // pieces, 4 * D * (i + 1) // pieces)
                nc.sync.dma_start(out=dst[:, cols], in_=view[:, cols])

        def load_wv(s, gp, pieces):
            load_rows(wv_sb[s][:, 4 * D * gp : 4 * D * (gp + 1)], Wv[s, 512 * gp : 512 * (gp + 1), :], pieces)

        def load_w1(s):
            nc.sync.dma_start(out=w1_sb[s][:], in_=W1[s].rearrange("(m a) k -> m (a k)", a=2))

        def load_subnet(s, pieces):
            wv_tile = raw.tile([P, 8 * D], BF16, tag="wv_sb")
            w1_tile = raw.tile([P, 2 * (D + DV)], BF16, tag="w1_sb")
            wv_sb.append(wv_tile)
            w1_sb.append(w1_tile)
            load_wv(s, 0, pieces)
            load_wv(s, 1, pieces)
            load_w1(s)

        load_rows(h_sb, h.flatten_outer_dims(), 2)
        load_subnet(0, 2)
        load_rows(x_sb, x.flatten_outer_dims(), 1)
        load_subnet(1, 1)
        load_subnet(2, 1)

        ident = const.tile([P, P], F32, name="ident")
        make_identity(nc, ident[:])
        zero = const.tile([P, 1], F32, name="zero")
        nc.vector.memset(zero[:], 0.0)
        warm = const.tile([P, 1], F32, name="warm")
        nc.scalar.activation(out=warm[:], in_=zero[:], func=SILU)

        def copy_out(engine, dst, src):
            if engine == "V":
                nc.vector.tensor_copy(out=dst, in_=src)
            else:
                nc.scalar.copy(out=dst, in_=src)

        def do(jobs, n):
            for job in jobs.get(n, []):
                job()

        def reorder(key, halves):
            if key not in ready:
                ready[key] = ordered.tile([P, 4096], BF16, tag="dst", align_bytes=64, name="dst")
            for half in halves:
                reordered.add((key, half))
                nc.vector.tensor_copy(
                    out=ready[key][:, 2048 * half : 2048 * (half + 1)]
                    .bitcast(F32)
                    .rearrange("p (u i w) -> p u i w", u=2, i=2),
                    in_=raw_half(key, half).bitcast(F32).rearrange("p i (w u) -> p u i w", u=2),
                )

        def transpose_half(src, step, half, key, engines, jobs):
            words = src.bitcast(F32)
            if half == 0:
                grouped_of[key] = stage.tile([P, 4096], BF16, tag="grouped", align_bytes=64, name="grouped")
            grouped_words = grouped_of[key][:].bitcast(F32)
            banks = [psum.tile([P, 512], F32, tag="bank", name="bank") for g in range(2)]
            order = [(i, g) for i in range(2) for g in range(2)] if step == 2 else [(i, g) for g in range(2) for i in range(2)]

            def empty(g):
                slot = 2 * half + g if key[0] == "w1" else half + 2 * g
                copy_out(
                    engines[2 * half + g],
                    grouped_words[:, 512 * slot : 512 * (slot + 1)].rearrange("p (c u) -> p c u", u=2),
                    banks[g][:].rearrange("p (u c) -> p c u", u=2),
                )
                do(jobs, 2 * half + g)

            for i, g in order:
                for u in range(2):
                    c0 = 256 * u + 128 * i
                    if step == 2:
                        w0 = (512 * half + 1024 * i if key[0] == "w1" else 1024 * half + 512 * i) + 256 * g
                        cols = slice(w0 + u, w0 + 256, 2)
                    else:
                        w0 = 1024 * half + 512 * u + 256 * i + 128 * g
                        cols = slice(w0, w0 + 128)
                    nc.tensor.transpose(banks[g][:, c0 : c0 + 128], words[:, cols], ident[:])
                if i == 1:
                    empty(g)

        def quantise(key, slots):
            if key in quantised:
                codes, scales = quantised[key]
            elif key[0] == "wv":
                codes = pair.tile([P, 1024], U32, tag="wv_codes%d" % key[2], align_bytes=64)
                scales = pair.tile([P, 1024], U8, tag="wv_scales%d" % key[2], align_bytes=64)
            elif key[0] == "w1":
                codes = pair.tile([P, 1024], U32, tag="w1_codes", align_bytes=64)
                scales = pair.tile([P, 1024], U8, tag="w1_scales", align_bytes=64)
            else:
                codes = keep.tile([P, 1024], U32, tag="%s_codes" % key[0], align_bytes=64)
                scales = keep.tile([P, 1024], U8, tag="%s_scales" % key[0], align_bytes=64)
            quantised[key] = (codes, scales)
            for slot in [None] if slots is None else slots:
                cols, values = (slice(0, 1024), slice(0, 4096)) if slot is None else (slice(256 * slot, 256 * (slot + 1)), slice(1024 * slot, 1024 * (slot + 1)))
                nc.vector.quantize_mx(
                    out=codes[:, cols].bitcast(FP8X4), scales=scales[:, cols], in_=grouped_of[key][:, values]
                )

        ready = {}
        reordered = set()
        grouped_of = {}
        quantised = {}
        views_grouped = {}
        views_q = {}

        def raw_of(key):
            if key[0] == "h":
                return h_sb[:]
            if key[0] == "x":
                return x_sb[:]
            if key[0] == "w1":
                return w1_sb[key[1]][:]
            return wv_sb[key[1]][:, 4 * D * key[2] : 4 * D * (key[2] + 1)]

        def raw_half(key, half):
            if key[0] == "w1":
                return raw_of(key).rearrange("p (a k) -> p a k", a=2)[:, :, D * half : D * (half + 1)]
            return raw_of(key)[:, 2 * D * half : 2 * D * (half + 1)].rearrange("p (i k) -> p i k", i=2)

        def T(key, engines, jobs, halves=(0, 1)):
            for half in halves:
                src, step = (ready[key][:], 1) if (key, half) in reordered else (raw_of(key), 2)
                transpose_half(src, step, half, key, engines, jobs)

        def perm(key, halves=(0, 1)):
            return lambda: reorder(key, halves)

        def quant(key, slots=None):
            return lambda: quantise(key, slots)

        def quantise_views(s, gp, j0, j1):
            v_codes, v_scales = views_q[(s, gp)]
            nc.vector.quantize_mx(
                out=v_codes[:, 128 * j0 : 128 * j1].bitcast(FP8X4),
                scales=v_scales[:, 128 * j0 : 128 * j1],
                in_=views_grouped[(s, gp)][:, 512 * j0 : 512 * j1],
            )

        def quant_views(s, gp, j0=0, j1=4):
            return lambda: quantise_views(s, gp, j0, j1)

        def views_tile(s, gp):
            v_grouped = pair.tile([P, 2048], BF16, tag="v_grouped%d" % gp, align_bytes=64)
            v_codes = pair.tile([P, 512], U32, tag="v_codes%d" % gp, align_bytes=64)
            v_scales = pair.tile([P, 512], U8, tag="v_scales%d" % gp, align_bytes=64)
            views_grouped[(s, gp)] = v_grouped
            views_q[(s, gp)] = (v_codes, v_scales)

        def views_bank(s, gp, j, engine):
            wv_codes, wv_scales = quantised[("wv", s, gp)]
            h_codes, h_scales = quantised[("h",)]
            v_grouped = views_grouped[(s, gp)]
            bank = psum.tile([P, 512], F32, tag="bank")
            for t in range(4):
                for g in range(2):
                    wc = slice(512 * g + 128 * t, 512 * g + 128 * (t + 1))
                    hc = slice(512 * g + 128 * j, 512 * g + 128 * (j + 1))
                    nc.tensor.matmul_mx(
                        out=bank[:, 128 * t : 128 * (t + 1)],
                        lhsT=wv_codes[:, wc].bitcast(FP8X4),
                        lhsT_scale=wv_scales[:, wc],
                        rhs=h_codes[:, hc].bitcast(FP8X4),
                        rhs_scale=h_scales[:, hc],
                        start=(g == 0),
                        stop=(g == 1),
                    )
            copy_out(
                engine,
                v_grouped[:, 512 * j : 512 * (j + 1)].rearrange("p (c t) -> p c t", t=4),
                bank[:].rearrange("p (t c) -> p c t", t=4),
            )

        def V(s, gp, engines, jobs):
            views_tile(s, gp)
            for j in range(4):
                views_bank(s, gp, j, engines[j])
                do(jobs, j)

        def out_view(s):
            return out[s].rearrange("b q f -> (b q) f").rearrange("(m j) f -> m (j f)", j=4)

        def out_passes(s, j, dst):
            w1_codes, w1_scales = quantised[("w1", s)]
            x_codes, x_scales = quantised[("x",)]
            operands = [(x_codes, x_scales, 512 * g + 128 * j) for g in range(2)]
            operands.extend([views_q[(s, gp)] + (128 * j,) for gp in range(2)])
            for n, (codes, scales, col) in enumerate(operands):
                nc.tensor.matmul_mx(
                    out=dst,
                    lhsT=codes[:, col : col + 128].bitcast(FP8X4),
                    lhsT_scale=scales[:, col : col + 128],
                    rhs=w1_codes[:, 256 * n : 256 * (n + 1)].bitcast(FP8X4),
                    rhs_scale=w1_scales[:, 256 * n : 256 * (n + 1)],
                    start=(n == 0),
                    stop=(n == 3),
                )

        def O(s, jobs):
            o_sb = pair.tile([P, 4 * SD], F32, tag="o_sb")
            for half in range(2):
                bank = psum.tile([P, 512], F32, tag="bank")
                for e in range(2):
                    out_passes(s, 2 * half + e, bank[:, 256 * e : 256 * (e + 1)])
                cols = slice(512 * half, 512 * (half + 1))
                nc.scalar.activation(
                    out=o_sb[:, cols].rearrange("p (j m a) -> p j m a", j=2, a=2),
                    in_=bank[:].rearrange("p (j a m) -> p j m a", j=2, a=2),
                    func=SILU,
                )
                do(jobs, half)
            nc.sync.dma_start(out=out_view(s), in_=o_sb[:])

        def O_fine(s, j, o_sb):
            bank = psum.tile([P, 512], F32, tag="bank")
            out_passes(s, j, bank[:, 0:256])
            cols = slice(256 * j, 256 * (j + 1))
            nc.scalar.activation(
                out=o_sb[:, cols].rearrange("p (m a) -> p m a", a=2),
                in_=bank[:, 0:256].rearrange("p (a m) -> p m a", a=2),
                func=SILU,
            )
            nc.sync.dma_start(out=out_view(s)[:, cols], in_=o_sb[:, cols])

        H, X = ("h",), ("x",)
        W00, W01, W10, W11 = [("wv", s, gp) for s in range(2) for gp in range(2)]
        A0, A1 = ("w1", 0), ("w1", 1)
        T(H, "VSSS", {})
        T(W00, "VSSS", {0: [quant(H)]})
        T(W01, "SSSS", {0: [quant(W00)]})
        V(0, 0, "SSSS", {0: [quant(W01)], 1: [perm(X)]})
        T(A0, "SSSS", {})
        V(0, 1, "SSSS", {0: [quant_views(0, 0), perm(W10), quant(A0)], 3: [perm(W11)]})
        T(X, "SVSS", {3: [quant_views(0, 1)]})
        load_subnet(3, 1)
        T(W10, "SSSV", {0: [quant(X)]})
        T(W11, "SSSS", {0: [perm(A1)]})
        O(0, {0: [quant(W10)]})
        T(A1, "VSVS", {1: [quant(W11)]})
        for s in range(1, NS):
            if s > 1:
                O(s - 1, {0: [quant(("wv", s, 1))]})
                T(("w1", s), "SSSV", {})
            V(s, 0, "SSSS", {0: [quant(("w1", s))], 1: [perm(("wv", s + 1, 0))] if s < NS - 1 else []})
            if s < NS - 1:
                V(s, 1, "SSSS", {0: [quant_views(s, 0)], 1: [perm(("wv", s + 1, 1))]})
                T(("wv", s + 1, 0), "VSVS", {0: [quant_views(s, 1)], 1: [perm(("w1", s + 1))]})
                T(("wv", s + 1, 1), "VSSS", {0: [quant(("wv", s + 1, 0))]})
        s = NS - 1
        o_sb = pair.tile([P, 4 * SD], F32, tag="o_sb")
        V(s, 1, "SSSV", {0: [quant_views(s, 0)], 1: [quant_views(s, 1, 0, 1)], 2: [quant_views(s, 1, 1, 2)], 3: [quant_views(s, 1, 2, 3), quant_views(s, 1, 3, 4)]})
        for j in range(4):
            O_fine(s, j, o_sb)
